import numpy as np
import ml_dtypes


def mxq(x, axis, fmt="e4m3"):
    dtype, down = {"e4m3": (ml_dtypes.float8_e4m3fn, 7), "e5m2": (ml_dtypes.float8_e5m2, 14)}[fmt]
    v = np.moveaxis(np.asarray(x, np.float32).astype(ml_dtypes.bfloat16).astype(np.float64), axis, -1)
    blocks = v.reshape(v.shape[:-1] + (-1, 32))
    amax = np.abs(blocks).max(-1, keepdims=True)
    byte = np.maximum(np.where(amax > 0, np.frexp(amax)[1] - 1 + 127, 0) - down, 1)
    scale = np.exp2(byte - 127.0)
    codes = (blocks / scale).astype(np.float32).astype(dtype).astype(np.float64)
    return np.moveaxis((codes * scale).reshape(v.shape), -1, axis)


WIDE = False


def mx_kscale(k):
    if not WIDE:
        return np.ones(k)
    levels = np.array([10, -10, 5, -5, 0])
    a = np.random.permutation(np.resize(levels, k // 512 * 4)).reshape(k // 512, 4)
    idx = np.arange(k)
    return np.exp2(a[idx // 512, idx % 128 // 32])


BF16 = ml_dtypes.bfloat16


def bf(x):
    return np.asarray(x, np.float32).astype(BF16)


def f64(x):
    return np.asarray(x).astype(np.float64)


B, C, H, W, M, O = 5, 512, 16, 16, 512, 512
N = B * H * W
L2_EPS = 1e-12
BN_EPS = 1e-5


def l2_normalize(x, axis):
    n = np.sqrt(np.sum(x * x, axis=axis, keepdims=True))
    return x / np.maximum(n, L2_EPS)


def setup_inputs():
    s = mx_kscale(C)
    cm = (np.random.standard_normal((N, C)) * 5.0 + np.random.standard_normal((1, C)) * 1.5) / np.sqrt(C)
    w = np.random.standard_normal((O, 2 * C)) * 0.1 / np.sqrt(2 * C)
    w[:, C:] = w[:, C:] / s
    return {"query": bf(np.random.standard_normal((B, C, H, W))), "concat_memory": bf(cm * s), "conv_w": bf(w),
            "bn_gamma": bf(1.0 + 0.1 * np.random.standard_normal(O)), "bn_beta": bf(0.2 * np.random.standard_normal(O))}


def reference(query, concat_memory, conv_w, bn_gamma, bn_beta):
    q_flat = l2_normalize(f64(query), 1).transpose(0, 2, 3, 1).reshape(N, C)
    upd = np.concatenate([q_flat, f64(concat_memory)], axis=1)
    y = mxq(upd, 1, "e4m3") @ mxq(f64(conv_w), 1, "e4m3").T
    y = y.reshape(B, H, W, O).transpose(0, 3, 1, 2)
    mean = np.mean(y, axis=(0, 2, 3), keepdims=True)
    var = np.mean((y - mean) ** 2, axis=(0, 2, 3), keepdims=True)
    y = (y - mean) / np.sqrt(var + BN_EPS)
    y = y * f64(bn_gamma)[None, :, None, None] + f64(bn_beta)[None, :, None, None]
    return np.maximum(y, 0.0)

@@ -1,0 +1,163 @@
+from contextlib import ExitStack
+
+import concourse.mybir as mybir
+from concourse.masks import make_identity
+
+F32 = mybir.dt.float32
+BF16 = mybir.dt.bfloat16
+U32 = mybir.dt.uint32
+U8 = mybir.dt.uint8
+FP8X4 = mybir.dt.float8_e4m3fn_x4
+ACT = mybir.ActivationFunctionType
+ALU = mybir.AluOpType
+
+P = 128
+B, C, HW, O = 5, 512, 256, 512
+NPIX = B * HW
+OT = O // P
+FLOPS = 2 * NPIX * 2 * C * O
+CHUNKS = ((0, 512), (512, 512), (1024, 256))
+
+
+def tile_memory_sup_pb_kernel(tc, query, concat_memory, conv_w, bn_gamma, bn_beta, out):
+    nc = tc.nc
+    with ExitStack() as ctx:
+        keep = ctx.enter_context(tc.tile_pool(name="keep", bufs=1))
+        psum = ctx.enter_context(tc.psum_pool(name="psum", bufs=8))
+
+        eps = keep.tile([P, 1], F32, name="eps")
+        nc.vector.memset(eps[:], 1e-5)
+        warm = keep.tile([P, 1], F32, name="warm")
+        nc.scalar.activation(out=warm[:], in_=eps[:], func=ACT.Abs_reciprocal_sqrt)
+        ones = keep.tile([P, P], F32, name="ones")
+        nc.vector.memset(ones[:], 1.0)
+        gb = keep.tile([P, P], BF16, name="gb")
+        nc.vector.memset(gb[:], 0.0)
+        ident = keep.tile([P, P], F32, name="ident")
+        make_identity(nc, ident[:])
+
+        q_view = query.rearrange("b (p j) h w -> p b j (h w)", j=4)
+        q_raw = []
+        for b in range(B):
+            t_q = keep.tile([P, 4, HW], BF16, name="q_raw%d" % b)
+            nc.sync.dma_start(out=t_q[:], in_=q_view[:, b, :, :])
+            q_raw.append(t_q)
+        cm_view = concat_memory.rearrange("(r p) c -> p r c", p=P)
+        cm_raw = []
+        for g in range(B):
+            t_c = keep.tile([P, 2, C], BF16, name="cm_raw%d" % g)
+            nc.sync.dma_start(out=t_c[:], in_=cm_view[:, 2 * g : 2 * g + 2, :])
+            cm_raw.append(t_c)
+        w_view = conv_w.rearrange("(t p) k -> p t k", p=P)
+        w_raw = []
+        for t in range(OT):
+            t_w = keep.tile([P, 2 * C], BF16, name="w_raw%d" % t)
+            nc.sync.dma_start(out=t_w[:], in_=w_view[:, t, :])
+            w_raw.append(t_w)
+        nc.sync.dma_start(out=gb[0:4, :], in_=bn_gamma.rearrange("(t p) -> t p", p=P))
+        nc.sync.dma_start(out=gb[4:8, :], in_=bn_beta.rearrange("(t p) -> t p", p=P))
+
+        u_codes = keep.tile([P, 2, NPIX], U32, name="u_codes", align_bytes=64)
+        u_scales = keep.tile([P, 2, NPIX], U8, name="u_scales", align_bytes=64)
+        w_codes = keep.tile([P, OT, 2 * P], U32, name="w_codes", align_bytes=64)
+        w_scales = keep.tile([P, OT, 2 * P], U8, name="w_scales", align_bytes=64)
+
+        for b in range(B):
+            cols = slice(b * HW, (b + 1) * HW)
+            sq = keep.tile([P, 4, HW], F32, name="sq%d" % b)
+            nc.scalar.activation(out=sq[:], in_=q_raw[b][:], func=ACT.Square)
+            sqp = keep.tile([P, 2, HW], F32, name="sqp%d" % b)
+            nc.vector.tensor_tensor(out=sqp[:], in0=sq[:, 0:2, :], in1=sq[:, 2:4, :], op=ALU.add)
+            ss = psum.tile([P, 512], F32, name="ss%d" % b, tag="bank")
+            nc.tensor.matmul(out=ss[:, 0:HW], lhsT=ones[:], rhs=sqp[:, 0, :], start=True, stop=False)
+            nc.tensor.matmul(out=ss[:, 0:HW], lhsT=ones[:], rhs=sqp[:, 1, :], start=False, stop=True)
+            rn = keep.tile([P, HW], F32, name="rn%d" % b)
+            nc.scalar.activation(out=rn[:], in_=ss[:, 0:HW], func=ACT.Abs_reciprocal_sqrt)
+            qg = keep.tile([P, HW, 4], BF16, name="qg%d" % b, align_bytes=64)
+            nc.vector.scalar_tensor_tensor(
+                out=qg[:],
+                in0=rn[:].unsqueeze(2).to_broadcast([P, HW, 4]),
+                scalar=1e12,
+                in1=q_raw[b][:].rearrange("p j w -> p w j"),
+                op0=ALU.min,
+                op1=ALU.mult,
+            )
+            nc.vector.quantize_mx(
+                out=u_codes[:, 0, cols].bitcast(FP8X4),
+                scales=u_scales[:, 0, cols],
+                in_=qg[:].rearrange("p w j -> p (w j)"),
+            )
+
+        for g in range(B):
+            cols = slice(g * HW, (g + 1) * HW)
+            cw = cm_raw[g][:].bitcast(F32)
+            c_t = psum.tile([P, 2, 2, P], F32, name="c_t%d" % g, tag="bank")
+            for r in range(2):
+                for u in range(2):
+                    nc.tensor.transpose(c_t[:, r, u, :], cw[:, r, u * P : (u + 1) * P], ident[:])
+            cg = keep.tile([P, 2, P, 4], BF16, name="cg%d" % g, align_bytes=64)
+            nc.scalar.copy(out=cg[:].bitcast(F32), in_=c_t[:].rearrange("p r u x -> p r x u"))
+            nc.vector.quantize_mx(
+                out=u_codes[:, 1, cols].bitcast(FP8X4),
+                scales=u_scales[:, 1, cols],
+                in_=cg[:].rearrange("p r x j -> p (r x j)"),
+            )
+
+        for t in range(OT):
+            ww = w_raw[t][:].bitcast(F32)
+            w_t = psum.tile([P, 2, 2, P], F32, name="w_t%d" % t, tag="bank")
+            for h in range(2):
+                nc.tensor.transpose(w_t[:, 0, h, :], ww[:, h : 2 * P : 2], ident[:])
+            for u in range(2):
+                nc.tensor.transpose(w_t[:, 1, u, :], ww[:, (2 + u) * P : (3 + u) * P], ident[:])
+            wg = keep.tile([P, 2, P, 4], BF16, name="wg%d" % t, align_bytes=64)
+            nc.scalar.copy(out=wg[:].bitcast(F32), in_=w_t[:].rearrange("p c u o -> p c o u"))
+            nc.vector.quantize_mx(
+                out=w_codes[:, t, :].bitcast(FP8X4),
+                scales=w_scales[:, t, :],
+                in_=wg[:].rearrange("p c o j -> p (c o j)"),
+            )
+
+        gbf = keep.tile([P, P], F32, name="gbf")
+        nc.vector.tensor_copy(out=gbf[:], in_=gb[:])
+        g_t = psum.tile([P, 512], F32, name="g_t", tag="bank")
+        nc.tensor.transpose(g_t[:, 0:P], gbf[:], ident[:])
+        gbt = keep.tile([P, 8], F32, name="gbt")
+        nc.vector.tensor_copy(out=gbt[:], in_=g_t[:, 0:8])
+
+        for t in range(OT):
+            stats = keep.tile([P, 3, 6], F32, name="stats%d" % t)
+            ys = []
+            for i, (c0, n) in enumerate(CHUNKS):
+                y = psum.tile([P, 512], F32, name="y%d_%d" % (t, i), tag="bank")
+                for c in range(2):
+                    nc.tensor.matmul_mx(
+                        out=y[:, 0:n],
+                        lhsT=w_codes[:, t, c * P : (c + 1) * P].bitcast(FP8X4),
+                        lhsT_scale=w_scales[:, t, c * P : (c + 1) * P],
+                        rhs=u_codes[:, c, c0 : c0 + n].bitcast(FP8X4),
+                        rhs_scale=u_scales[:, c, c0 : c0 + n],
+                        start=(c == 0),
+                        stop=(c == 1),
+                    )
+                nc.vector.bn_stats(out=stats[:, i, :], in_=y[:, 0:n])
+                ys.append(y)
+            mv = keep.tile([P, 2], F32, name="mv%d" % t)
+            nc.vector.bn_aggr(out=mv[:], in_=stats[:].rearrange("p a s -> p (a s)"))
+            rstd = keep.tile([P, 1], F32, name="rstd%d" % t)
+            nc.scalar.activation(out=rstd[:], in_=mv[:, 1:2], func=ACT.Abs_reciprocal_sqrt, bias=eps[:])
+            scl = keep.tile([P, 1], F32, name="scl%d" % t)
+            nc.vector.tensor_tensor(out=scl[:], in0=gbt[:, t : t + 1], in1=rstd[:], op=ALU.mult)
+            tmp = keep.tile([P, 1], F32, name="tmp%d" % t)
+            nc.vector.tensor_tensor(out=tmp[:], in0=mv[:, 0:1], in1=scl[:], op=ALU.mult)
+            shift = keep.tile([P, 1], F32, name="shift%d" % t)
+            nc.vector.tensor_tensor(out=shift[:], in0=gbt[:, 4 + t : 5 + t], in1=tmp[:], op=ALU.subtract)
+            res = keep.tile([P, NPIX], F32, name="res%d" % t)
+            for i, (c0, n) in enumerate(CHUNKS):
+                nc.scalar.activation(
+                    out=res[:, c0 : c0 + n], in_=ys[i][:, 0:n], func=ACT.Relu, bias=shift[:], scale=scl[:]
+                )
+            nc.sync.dma_start(
+                out=out[:, t * P : (t + 1) * P, :, :].rearrange("b p h w -> p b (h w)"),
+                in_=res[:].rearrange("p (b x) -> p b x", b=B),
+            )

@@ -24,140 +24,248 @@ def tile_memory_sup_pb_kernel(tc, query, concat_memory, conv_w, bn_gamma, bn_bet
     with ExitStack() as ctx:
         keep = ctx.enter_context(tc.tile_pool(name="keep", bufs=1))
         psum = ctx.enter_context(tc.psum_pool(name="psum", bufs=8))
+        ctx.enter_context(tc.manual_schedule())
 
-        eps = keep.tile([P, 1], F32, name="eps")
-        nc.vector.memset(eps[:], 1e-5)
-        warm = keep.tile([P, 1], F32, name="warm")
-        nc.scalar.activation(out=warm[:], in_=eps[:], func=ACT.Abs_reciprocal_sqrt)
-        ones = keep.tile([P, P], F32, name="ones")
-        nc.vector.memset(ones[:], 1.0)
+        one1 = keep.tile([P, 1], F32, name="one1")
+        nc.vector.memset(one1[:], 1.0)
         gb = keep.tile([P, P], BF16, name="gb")
         nc.vector.memset(gb[:], 0.0)
         ident = keep.tile([P, P], F32, name="ident")
         make_identity(nc, ident[:])
+        nc.scalar.dma_start(out=gb[0:4, :], in_=bn_gamma.rearrange("(t p) -> t p", p=P))
+        nc.scalar.dma_start(out=gb[4:8, :], in_=bn_beta.rearrange("(t p) -> t p", p=P))
+        warm = keep.tile([P, 1], F32, name="warm")
+        nc.scalar.activation(out=warm[:], in_=one1[:], func=ACT.Abs_reciprocal_sqrt)
 
         q_view = query.rearrange("b (p j) h w -> p b j (h w)", j=4)
-        q_raw = []
-        for b in range(B):
-            t_q = keep.tile([P, 4, HW], BF16, name="q_raw%d" % b)
-            nc.sync.dma_start(out=t_q[:], in_=q_view[:, b, :, :])
-            q_raw.append(t_q)
         cm_view = concat_memory.rearrange("(r p) c -> p r c", p=P)
-        cm_raw = []
-        for g in range(B):
-            t_c = keep.tile([P, 2, C], BF16, name="cm_raw%d" % g)
-            nc.sync.dma_start(out=t_c[:], in_=cm_view[:, 2 * g : 2 * g + 2, :])
-            cm_raw.append(t_c)
         w_view = conv_w.rearrange("(t p) k -> p t k", p=P)
-        w_raw = []
-        for t in range(OT):
-            t_w = keep.tile([P, 2 * C], BF16, name="w_raw%d" % t)
-            nc.sync.dma_start(out=t_w[:], in_=w_view[:, t, :])
-            w_raw.append(t_w)
-        nc.sync.dma_start(out=gb[0:4, :], in_=bn_gamma.rearrange("(t p) -> t p", p=P))
-        nc.sync.dma_start(out=gb[4:8, :], in_=bn_beta.rearrange("(t p) -> t p", p=P))
+        q_raw = [keep.tile([P, 4, HW], BF16, name="q_raw%d" % b) for b in range(B)]
+        cm_raw = [keep.tile([P, 2, C], BF16, name="cm_raw%d" % g) for g in range(B)]
+        w_raw = [keep.tile([P, 2 * C], BF16, name="w_raw%d" % t) for t in range(OT)]
+
+        def load_q(b):
+            nc.sync.dma_start(out=q_raw[b][:], in_=q_view[:, b, :, :])
+
+        def load_cm(g):
+            nc.sync.dma_start(out=cm_raw[g][:], in_=cm_view[:, 2 * g : 2 * g + 2, :])
+
+        def load_w(t):
+            nc.sync.dma_start(out=w_raw[t][:], in_=w_view[:, t, :])
+
+        load_q(0)
+        load_w(0)
+        load_cm(0)
+        for b in range(1, B):
+            load_q(b)
+            load_cm(b)
+        for t in range(1, OT):
+            load_w(t)
 
         u_codes = keep.tile([P, 2, NPIX], U32, name="u_codes", align_bytes=64)
         u_scales = keep.tile([P, 2, NPIX], U8, name="u_scales", align_bytes=64)
         w_codes = keep.tile([P, OT, 2 * P], U32, name="w_codes", align_bytes=64)
         w_scales = keep.tile([P, OT, 2 * P], U8, name="w_scales", align_bytes=64)
+        junk = keep.tile([P, 4, P], BF16, name="junk")
+        tq, ss, rn, r_t, qg = {}, {}, {}, {}, {}
+        c_t, cg, w_t, wg = {}, {}, {}, {}
 
-        for b in range(B):
-            cols = slice(b * HW, (b + 1) * HW)
-            sq = keep.tile([P, 4, HW], F32, name="sq%d" % b)
-            nc.scalar.activation(out=sq[:], in_=q_raw[b][:], func=ACT.Square)
-            sqp = keep.tile([P, 2, HW], F32, name="sqp%d" % b)
-            nc.vector.tensor_tensor(out=sqp[:], in0=sq[:, 0:2, :], in1=sq[:, 2:4, :], op=ALU.add)
-            ss = psum.tile([P, 512], F32, name="ss%d" % b, tag="bank")
-            nc.tensor.matmul(out=ss[:, 0:HW], lhsT=ones[:], rhs=sqp[:, 0, :], start=True, stop=False)
-            nc.tensor.matmul(out=ss[:, 0:HW], lhsT=ones[:], rhs=sqp[:, 1, :], start=False, stop=True)
-            rn = keep.tile([P, HW], F32, name="rn%d" % b)
-            nc.scalar.activation(out=rn[:], in_=ss[:, 0:HW], func=ACT.Abs_reciprocal_sqrt)
-            qg = keep.tile([P, HW, 4], BF16, name="qg%d" % b, align_bytes=64)
+        def t_q(b):
+            tq[b] = psum.tile([P, 4, P], F32, name="tq%d" % b, tag="bank")
+            qw = q_raw[b][:].bitcast(F32)
+            for j in range(4):
+                nc.tensor.transpose(tq[b][:, j, :], qw[:, j, :], ident[:])
+
+        def sq_q(b):
+            ss[b] = keep.tile([P, 2], F32, name="ss%d" % b)
+            v = tq[b][:].bitcast(BF16).rearrange("p j (c e) -> p e j c", e=2)
+            for e in range(2):
+                nc.scalar.activation(out=junk[:], in_=v[:, e, :, :], func=ACT.Square, accum_out=ss[b][:, e : e + 1])
+            rn[b] = keep.tile([P, 2], F32, name="rn%d" % b)
+            nc.scalar.activation(out=rn[b][:], in_=ss[b][:], func=ACT.Abs_reciprocal_sqrt)
+
+        def bc_q(b):
+            r_t[b] = psum.tile([P, 512], F32, name="r_t%d" % b, tag="bank")
+            for e in range(2):
+                nc.tensor.matmul(
+                    out=r_t[b][:, e:HW:2],
+                    lhsT=rn[b][:, e : e + 1].to_broadcast([P, P]),
+                    rhs=ident[:],
+                    start=True,
+                    stop=True,
+                )
+
+        def st_q(b):
+            qg[b] = keep.tile([P, HW, 4], BF16, name="qg%d" % b, align_bytes=64)
             nc.vector.scalar_tensor_tensor(
-                out=qg[:],
-                in0=rn[:].unsqueeze(2).to_broadcast([P, HW, 4]),
+                out=qg[b][:],
+                in0=r_t[b][:, 0:HW].unsqueeze(2).to_broadcast([P, HW, 4]),
                 scalar=1e12,
                 in1=q_raw[b][:].rearrange("p j w -> p w j"),
                 op0=ALU.min,
                 op1=ALU.mult,
             )
+
+        def qq(b):
+            cols = slice(b * HW, (b + 1) * HW)
             nc.vector.quantize_mx(
                 out=u_codes[:, 0, cols].bitcast(FP8X4),
                 scales=u_scales[:, 0, cols],
-                in_=qg[:].rearrange("p w j -> p (w j)"),
+                in_=qg[b][:].rearrange("p w j -> p (w j)"),
             )
 
-        for g in range(B):
-            cols = slice(g * HW, (g + 1) * HW)
+        def t_c(g):
+            c_t[g] = psum.tile([P, 2, 2, P], F32, name="c_t%d" % g, tag="bank")
             cw = cm_raw[g][:].bitcast(F32)
-            c_t = psum.tile([P, 2, 2, P], F32, name="c_t%d" % g, tag="bank")
             for r in range(2):
                 for u in range(2):
-                    nc.tensor.transpose(c_t[:, r, u, :], cw[:, r, u * P : (u + 1) * P], ident[:])
-            cg = keep.tile([P, 2, P, 4], BF16, name="cg%d" % g, align_bytes=64)
-            nc.scalar.copy(out=cg[:].bitcast(F32), in_=c_t[:].rearrange("p r u x -> p r x u"))
+                    nc.tensor.transpose(c_t[g][:, r, u, :], cw[:, r, u * P : (u + 1) * P], ident[:])
+
+        def cp_c(g, on_vector):
+            cg[g] = keep.tile([P, 2, P, 4], BF16, name="cg%d" % g, align_bytes=64)
+            src = c_t[g][:].rearrange("p r u x -> p r x u")
+            if on_vector:
+                nc.vector.tensor_copy(out=cg[g][:].bitcast(F32), in_=src)
+            else:
+                nc.scalar.copy(out=cg[g][:].bitcast(F32), in_=src)
+
+        def qc(g):
+            cols = slice(g * HW, (g + 1) * HW)
             nc.vector.quantize_mx(
                 out=u_codes[:, 1, cols].bitcast(FP8X4),
                 scales=u_scales[:, 1, cols],
-                in_=cg[:].rearrange("p r x j -> p (r x j)"),
+                in_=cg[g][:].rearrange("p r x j -> p (r x j)"),
             )
 
-        for t in range(OT):
+        def t_w(t):
+            w_t[t] = psum.tile([P, 2, 2, P], F32, name="w_t%d" % t, tag="bank")
             ww = w_raw[t][:].bitcast(F32)
-            w_t = psum.tile([P, 2, 2, P], F32, name="w_t%d" % t, tag="bank")
             for h in range(2):
-                nc.tensor.transpose(w_t[:, 0, h, :], ww[:, h : 2 * P : 2], ident[:])
+                nc.tensor.transpose(w_t[t][:, 0, h, :], ww[:, h : 2 * P : 2], ident[:])
             for u in range(2):
-                nc.tensor.transpose(w_t[:, 1, u, :], ww[:, (2 + u) * P : (3 + u) * P], ident[:])
-            wg = keep.tile([P, 2, P, 4], BF16, name="wg%d" % t, align_bytes=64)
-            nc.scalar.copy(out=wg[:].bitcast(F32), in_=w_t[:].rearrange("p c u o -> p c o u"))
+                nc.tensor.transpose(w_t[t][:, 1, u, :], ww[:, (2 + u) * P : (3 + u) * P], ident[:])
+
+        def cp_w(t, on_vector):
+            wg[t] = keep.tile([P, 2, P, 4], BF16, name="wg%d" % t, align_bytes=64)
+            src = w_t[t][:].rearrange("p c u o -> p c o u")
+            if on_vector:
+                nc.vector.tensor_copy(out=wg[t][:].bitcast(F32), in_=src)
+            else:
+                nc.scalar.copy(out=wg[t][:].bitcast(F32), in_=src)
+
+        def quant_w(t):
             nc.vector.quantize_mx(
                 out=w_codes[:, t, :].bitcast(FP8X4),
                 scales=w_scales[:, t, :],
-                in_=wg[:].rearrange("p c o j -> p (c o j)"),
+                in_=wg[t][:].rearrange("p c o j -> p (c o j)"),
             )
 
+        t_q(0)
+        t_w(0)
+        t_c(0)
+        sq_q(0)
+        cp_w(0, True)
+        cp_c(0, True)
+        quant_w(0)
+        qc(0)
+        t_q(1)
+        bc_q(0)
+        t_c(1)
+        sq_q(1)
+        st_q(0)
+        t_q(2)
+        bc_q(1)
+        t_c(2)
+        sq_q(2)
+        st_q(1)
+        qq(0)
         gbf = keep.tile([P, P], F32, name="gbf")
         nc.vector.tensor_copy(out=gbf[:], in_=gb[:])
+        t_q(3)
+        bc_q(2)
+        t_c(3)
         g_t = psum.tile([P, 512], F32, name="g_t", tag="bank")
         nc.tensor.transpose(g_t[:, 0:P], gbf[:], ident[:])
+        sq_q(3)
+        st_q(2)
+        qq(1)
         gbt = keep.tile([P, 8], F32, name="gbt")
         nc.vector.tensor_copy(out=gbt[:], in_=g_t[:, 0:8])
+        t_q(4)
+        bc_q(3)
+        t_c(4)
+        t_w(1)
+        sq_q(4)
+        st_q(3)
+        qq(2)
+        bc_q(4)
+        t_w(2)
+        t_w(3)
+        st_q(4)
+        qq(3)
+        for g in range(1, B):
+            cp_c(g, False)
+        for t in range(1, OT):
+            cp_w(t, False)
+        qc(1)
+        qq(4)
+        qc(2)
+        qc(3)
+        qc(4)
+        quant_w(1)
+
+        ys, stats = {}, {}
+
+        def mx(t, i):
+            c0, n = CHUNKS[i]
+            ys[(t, i)] = psum.tile([P, 512], F32, name="y%d_%d" % (t, i), tag="bank")
+            for c in range(2):
+                nc.tensor.matmul_mx(
+                    out=ys[(t, i)][:, 0:n],
+                    lhsT=w_codes[:, t, c * P : (c + 1) * P].bitcast(FP8X4),
+                    lhsT_scale=w_scales[:, t, c * P : (c + 1) * P],
+                    rhs=u_codes[:, c, c0 : c0 + n].bitcast(FP8X4),
+                    rhs_scale=u_scales[:, c, c0 : c0 + n],
+                    start=(c == 0),
+                    stop=(c == 1),
+                )
+
+        def bs(t, i):
+            n = CHUNKS[i][1]
+            nc.vector.bn_stats(out=stats[t][:, i, :], in_=ys[(t, i)][:, 0:n])
 
         for t in range(OT):
-            stats = keep.tile([P, 3, 6], F32, name="stats%d" % t)
-            ys = []
-            for i, (c0, n) in enumerate(CHUNKS):
-                y = psum.tile([P, 512], F32, name="y%d_%d" % (t, i), tag="bank")
-                for c in range(2):
-                    nc.tensor.matmul_mx(
-                        out=y[:, 0:n],
-                        lhsT=w_codes[:, t, c * P : (c + 1) * P].bitcast(FP8X4),
-                        lhsT_scale=w_scales[:, t, c * P : (c + 1) * P],
-                        rhs=u_codes[:, c, c0 : c0 + n].bitcast(FP8X4),
-                        rhs_scale=u_scales[:, c, c0 : c0 + n],
-                        start=(c == 0),
-                        stop=(c == 1),
-                    )
-                nc.vector.bn_stats(out=stats[:, i, :], in_=y[:, 0:n])
-                ys.append(y)
+            stats[t] = keep.tile([P, 3, 6], F32, name="stats%d" % t)
+            for i in range(3):
+                mx(t, i)
+                bs(t, i)
+                if t == 0 and i < 2:
+                    quant_w(i + 2)
             mv = keep.tile([P, 2], F32, name="mv%d" % t)
-            nc.vector.bn_aggr(out=mv[:], in_=stats[:].rearrange("p a s -> p (a s)"))
+            nc.vector.bn_aggr(out=mv[:], in_=stats[t][:].rearrange("p a s -> p (a s)"))
+            ve = keep.tile([P, 1], F32, name="ve%d" % t)
+            nc.vector.tensor_scalar(out=ve[:], in0=mv[:, 1:2], scalar1=1e-5, scalar2=None, op0=ALU.add)
+            nm = keep.tile([P, 1], F32, name="nm%d" % t)
+            nc.vector.tensor_scalar(out=nm[:], in0=mv[:, 0:1], scalar1=-1.0, scalar2=None, op0=ALU.mult)
             rstd = keep.tile([P, 1], F32, name="rstd%d" % t)
-            nc.scalar.activation(out=rstd[:], in_=mv[:, 1:2], func=ACT.Abs_reciprocal_sqrt, bias=eps[:])
+            nc.scalar.activation(out=rstd[:], in_=ve[:], func=ACT.Abs_reciprocal_sqrt)
             scl = keep.tile([P, 1], F32, name="scl%d" % t)
-            nc.vector.tensor_tensor(out=scl[:], in0=gbt[:, t : t + 1], in1=rstd[:], op=ALU.mult)
-            tmp = keep.tile([P, 1], F32, name="tmp%d" % t)
-            nc.vector.tensor_tensor(out=tmp[:], in0=mv[:, 0:1], in1=scl[:], op=ALU.mult)
+            nc.scalar.activation(out=scl[:], in_=rstd[:], func=ACT.Copy, scale=gbt[:, t : t + 1])
             shift = keep.tile([P, 1], F32, name="shift%d" % t)
-            nc.vector.tensor_tensor(out=shift[:], in0=gbt[:, 4 + t : 5 + t], in1=tmp[:], op=ALU.subtract)
-            res = keep.tile([P, NPIX], F32, name="res%d" % t)
-            for i, (c0, n) in enumerate(CHUNKS):
-                nc.scalar.activation(
-                    out=res[:, c0 : c0 + n], in_=ys[i][:, 0:n], func=ACT.Relu, bias=shift[:], scale=scl[:]
-                )
-            nc.sync.dma_start(
-                out=out[:, t * P : (t + 1) * P, :, :].rearrange("b p h w -> p b (h w)"),
-                in_=res[:].rearrange("p (b x) -> p b x", b=B),
+            nc.scalar.activation(
+                out=shift[:], in_=nm[:], func=ACT.Identity, scale=scl[:], bias=gbt[:, 4 + t : 5 + t]
             )
+            for i in (0, 2, 1) if t == OT - 1 else (0, 1, 2):
+                c0, n = CHUNKS[i]
+                res = keep.tile([P, n], F32, name="res%d_%d" % (t, i))
+                if t == OT - 1 and i == 1:
+                    nc.vector.tensor_scalar(
+                        out=res[:], in0=ys[(t, i)][:, 0:n], scalar1=scl[:], scalar2=shift[:], op0=ALU.mult, op1=ALU.add
+                    )
+                    nc.vector.tensor_scalar(out=res[:], in0=res[:], scalar1=0.0, scalar2=None, op0=ALU.max)
+                else:
+                    nc.scalar.activation(out=res[:], in_=ys[(t, i)][:, 0:n], func=ACT.Relu, bias=shift[:], scale=scl[:])
+                nc.sync.dma_start(
+                    out=out[c0 // HW : (c0 + n) // HW, t * P : (t + 1) * P, :, :].rearrange("b p h w -> p b (h w)"),
+                    in_=res[:].rearrange("p (b x) -> p b x", x=HW),
+                )

@@ -28,6 +28,8 @@ def tile_memory_sup_pb_kernel(tc, query, concat_memory, conv_w, bn_gamma, bn_bet
 
         one1 = keep.tile([P, 1], F32, name="one1")
         nc.vector.memset(one1[:], 1.0)
+        eps = keep.tile([P, 1], F32, name="eps")
+        nc.vector.tensor_scalar(out=eps[:], in0=one1[:], scalar1=1e-5, scalar2=None, op0=ALU.mult)
         gb = keep.tile([P, P], BF16, name="gb")
         nc.vector.memset(gb[:], 0.0)
         ident = keep.tile([P, P], F32, name="ident")
@@ -55,10 +57,12 @@ def tile_memory_sup_pb_kernel(tc, query, concat_memory, conv_w, bn_gamma, bn_bet
 
         load_q(0)
         load_w(0)
+        load_q(1)
         load_cm(0)
-        for b in range(1, B):
+        for b in range(2, B):
             load_q(b)
-            load_cm(b)
+        for g in range(1, B):
+            load_cm(g)
         for t in range(1, OT):
             load_w(t)
 
@@ -162,51 +166,51 @@ def tile_memory_sup_pb_kernel(tc, query, concat_memory, conv_w, bn_gamma, bn_bet
 
         t_q(0)
         t_w(0)
+        t_q(1)
         t_c(0)
         sq_q(0)
         cp_w(0, True)
         cp_c(0, True)
         quant_w(0)
         qc(0)
-        t_q(1)
         bc_q(0)
-        t_c(1)
+        t_q(2)
         sq_q(1)
         st_q(0)
-        t_q(2)
         bc_q(1)
-        t_c(2)
+        t_q(3)
         sq_q(2)
         st_q(1)
         qq(0)
         gbf = keep.tile([P, P], F32, name="gbf")
         nc.vector.tensor_copy(out=gbf[:], in_=gb[:])
-        t_q(3)
         bc_q(2)
-        t_c(3)
-        g_t = psum.tile([P, 512], F32, name="g_t", tag="bank")
-        nc.tensor.transpose(g_t[:, 0:P], gbf[:], ident[:])
+        t_q(4)
         sq_q(3)
         st_q(2)
         qq(1)
-        gbt = keep.tile([P, 8], F32, name="gbt")
-        nc.vector.tensor_copy(out=gbt[:], in_=g_t[:, 0:8])
-        t_q(4)
         bc_q(3)
-        t_c(4)
-        t_w(1)
+        t_c(1)
         sq_q(4)
         st_q(3)
         qq(2)
         bc_q(4)
-        t_w(2)
-        t_w(3)
-        st_q(4)
-        qq(3)
+        for g in range(2, B):
+            t_c(g)
+        for t in range(1, OT):
+            t_w(t)
+        g_t = psum.tile([P, 512], F32, name="g_t", tag="bank")
+        nc.tensor.transpose(g_t[:, 0:P], gbf[:], ident[:])
         for g in range(1, B):
             cp_c(g, False)
         for t in range(1, OT):
             cp_w(t, False)
+        gbt = keep.tile([P, 8], F32, name="gbt")
+        nc.scalar.copy(out=gbt[:], in_=g_t[:, 0:8])
+        ngam = keep.tile([P, 4], F32, name="ngam")
+        nc.scalar.activation(out=ngam[:], in_=g_t[:, 0:4], func=ACT.Copy, scale=-1.0)
+        st_q(4)
+        qq(3)
         qc(1)
         qq(4)
         qc(2)
@@ -214,7 +218,7 @@ def tile_memory_sup_pb_kernel(tc, query, concat_memory, conv_w, bn_gamma, bn_bet
         qc(4)
         quant_w(1)
 
-        ys, stats = {}, {}
+        ys, stats, mv, rstd, nmg, scl, shift = {}, {}, {}, {}, {}, {}, {}
 
         def mx(t, i):
             c0, n = CHUNKS[i]
@@ -230,42 +234,65 @@ def tile_memory_sup_pb_kernel(tc, query, concat_memory, conv_w, bn_gamma, bn_bet
                     stop=(c == 1),
                 )
 
-        def bs(t, i):
-            n = CHUNKS[i][1]
-            nc.vector.bn_stats(out=stats[t][:, i, :], in_=ys[(t, i)][:, 0:n])
-
-        for t in range(OT):
+        def tile_stats(t):
             stats[t] = keep.tile([P, 3, 6], F32, name="stats%d" % t)
             for i in range(3):
                 mx(t, i)
-                bs(t, i)
-                if t == 0 and i < 2:
-                    quant_w(i + 2)
-            mv = keep.tile([P, 2], F32, name="mv%d" % t)
-            nc.vector.bn_aggr(out=mv[:], in_=stats[t][:].rearrange("p a s -> p (a s)"))
-            ve = keep.tile([P, 1], F32, name="ve%d" % t)
-            nc.vector.tensor_scalar(out=ve[:], in0=mv[:, 1:2], scalar1=1e-5, scalar2=None, op0=ALU.add)
-            nm = keep.tile([P, 1], F32, name="nm%d" % t)
-            nc.vector.tensor_scalar(out=nm[:], in0=mv[:, 0:1], scalar1=-1.0, scalar2=None, op0=ALU.mult)
-            rstd = keep.tile([P, 1], F32, name="rstd%d" % t)
-            nc.scalar.activation(out=rstd[:], in_=ve[:], func=ACT.Abs_reciprocal_sqrt)
-            scl = keep.tile([P, 1], F32, name="scl%d" % t)
-            nc.scalar.activation(out=scl[:], in_=rstd[:], func=ACT.Copy, scale=gbt[:, t : t + 1])
-            shift = keep.tile([P, 1], F32, name="shift%d" % t)
+                nc.vector.bn_stats(out=stats[t][:, i, :], in_=ys[(t, i)][:, 0 : CHUNKS[i][1]])
+
+        def aggr(t):
+            mv[t] = keep.tile([P, 2], F32, name="mv%d" % t)
+            nc.vector.bn_aggr(out=mv[t][:], in_=stats[t][:].rearrange("p a s -> p (a s)"))
+
+        def chain_a(t):
+            rstd[t] = keep.tile([P, 1], F32, name="rstd%d" % t)
+            nc.scalar.activation(out=rstd[t][:], in_=mv[t][:, 1:2], func=ACT.Abs_reciprocal_sqrt, bias=eps[:])
+            nmg[t] = keep.tile([P, 1], F32, name="nmg%d" % t)
+            nc.scalar.activation(out=nmg[t][:], in_=mv[t][:, 0:1], func=ACT.Copy, scale=ngam[:, t : t + 1])
+
+        def chain_b(t):
+            scl[t] = keep.tile([P, 1], F32, name="scl%d" % t)
+            nc.scalar.activation(out=scl[t][:], in_=rstd[t][:], func=ACT.Copy, scale=gbt[:, t : t + 1])
+            shift[t] = keep.tile([P, 1], F32, name="shift%d" % t)
             nc.scalar.activation(
-                out=shift[:], in_=nm[:], func=ACT.Identity, scale=scl[:], bias=gbt[:, 4 + t : 5 + t]
+                out=shift[t][:], in_=rstd[t][:], func=ACT.Identity, scale=nmg[t][:], bias=gbt[:, 4 + t : 5 + t]
             )
-            for i in (0, 2, 1) if t == OT - 1 else (0, 1, 2):
-                c0, n = CHUNKS[i]
-                res = keep.tile([P, n], F32, name="res%d_%d" % (t, i))
-                if t == OT - 1 and i == 1:
-                    nc.vector.tensor_scalar(
-                        out=res[:], in0=ys[(t, i)][:, 0:n], scalar1=scl[:], scalar2=shift[:], op0=ALU.mult, op1=ALU.add
-                    )
-                    nc.vector.tensor_scalar(out=res[:], in0=res[:], scalar1=0.0, scalar2=None, op0=ALU.max)
-                else:
-                    nc.scalar.activation(out=res[:], in_=ys[(t, i)][:, 0:n], func=ACT.Relu, bias=shift[:], scale=scl[:])
-                nc.sync.dma_start(
-                    out=out[c0 // HW : (c0 + n) // HW, t * P : (t + 1) * P, :, :].rearrange("b p h w -> p b (h w)"),
-                    in_=res[:].rearrange("p (b x) -> p b x", x=HW),
+
+        def relu(t, i, on_vector):
+            c0, n = CHUNKS[i]
+            res = keep.tile([P, n], F32, name="res%d_%d" % (t, i))
+            if on_vector:
+                nc.vector.tensor_scalar(
+                    out=res[:], in0=ys[(t, i)][:, 0:n], scalar1=scl[t][:], scalar2=shift[t][:], op0=ALU.mult, op1=ALU.add
                 )
+                nc.vector.tensor_scalar(out=res[:], in0=res[:], scalar1=0.0, scalar2=None, op0=ALU.max)
+            else:
+                nc.scalar.activation(out=res[:], in_=ys[(t, i)][:, 0:n], func=ACT.Relu, bias=shift[t][:], scale=scl[t][:])
+            nc.sync.dma_start(
+                out=out[c0 // HW : (c0 + n) // HW, t * P : (t + 1) * P, :, :].rearrange("b p h w -> p b (h w)"),
+                in_=res[:].rearrange("p (b x) -> p b x", x=HW),
+            )
+
+        tile_stats(0)
+        quant_w(2)
+        aggr(0)
+        chain_a(0)
+        chain_b(0)
+        tile_stats(1)
+        quant_w(3)
+        aggr(1)
+        for t in range(OT - 1):
+            relu(t, 0, False)
+            relu(t, 1, False)
+            chain_a(t + 1)
+            if t + 2 < OT:
+                relu(t, 2, False)
+                chain_b(t + 1)
+                tile_stats(t + 2)
+                aggr(t + 2)
+            else:
+                relu(t, 2, True)
+                chain_b(t + 1)
+        relu(OT - 1, 0, False)
+        relu(OT - 1, 2, False)
+        relu(OT - 1, 1, True)

@@ -30,6 +30,11 @@ def tile_memory_sup_pb_kernel(tc, query, concat_memory, conv_w, bn_gamma, bn_bet
         nc.vector.memset(one1[:], 1.0)
         eps = keep.tile([P, 1], F32, name="eps")
         nc.vector.tensor_scalar(out=eps[:], in0=one1[:], scalar1=1e-5, scalar2=None, op0=ALU.mult)
+        ones = keep.tile([P, P], F32, name="ones")
+        nc.vector.memset(ones[:], 1.0)
+        warm_ps = psum.tile([P, 512], F32, name="warm_ps", tag="bank")
+        for i in range(4):
+            nc.tensor.matmul(out=warm_ps[:, 0:P], lhsT=ones[:], rhs=ones[:], start=True, stop=True)
         gb = keep.tile([P, P], BF16, name="gb")
         nc.vector.memset(gb[:], 0.0)
         ident = keep.tile([P, P], F32, name="ident")
@@ -186,17 +191,18 @@ def tile_memory_sup_pb_kernel(tc, query, concat_memory, conv_w, bn_gamma, bn_bet
         nc.vector.tensor_copy(out=gbf[:], in_=gb[:])
         bc_q(2)
         t_q(4)
+        t_c(1)
         sq_q(3)
         st_q(2)
         qq(1)
         bc_q(3)
-        t_c(1)
+        t_c(2)
+        t_c(3)
         sq_q(4)
         st_q(3)
         qq(2)
         bc_q(4)
-        for g in range(2, B):
-            t_c(g)
+        t_c(4)
         for t in range(1, OT):
             t_w(t)
         g_t = psum.tile([P, 512], F32, name="g_t", tag="bank")
@@ -262,16 +268,29 @@ def tile_memory_sup_pb_kernel(tc, query, concat_memory, conv_w, bn_gamma, bn_bet
             c0, n = CHUNKS[i]
             res = keep.tile([P, n], F32, name="res%d_%d" % (t, i))
             if on_vector:
-                nc.vector.tensor_scalar(
-                    out=res[:], in0=ys[(t, i)][:, 0:n], scalar1=scl[t][:], scalar2=shift[t][:], op0=ALU.mult, op1=ALU.add
-                )
-                nc.vector.tensor_scalar(out=res[:], in0=res[:], scalar1=0.0, scalar2=None, op0=ALU.max)
+                for h in range(0, n, HW):
+                    nc.vector.tensor_scalar(
+                        out=res[:, h : h + HW],
+                        in0=ys[(t, i)][:, h : h + HW],
+                        scalar1=scl[t][:],
+                        scalar2=shift[t][:],
+                        op0=ALU.mult,
+                        op1=ALU.add,
+                    )
+                for h in range(0, n, HW):
+                    nc.vector.tensor_scalar(
+                        out=res[:, h : h + HW], in0=res[:, h : h + HW], scalar1=0.0, scalar2=None, op0=ALU.max
+                    )
+                    nc.sync.dma_start(
+                        out=out[(c0 + h) // HW, t * P : (t + 1) * P, :, :].rearrange("p h w -> p (h w)"),
+                        in_=res[:, h : h + HW],
+                    )
             else:
                 nc.scalar.activation(out=res[:], in_=ys[(t, i)][:, 0:n], func=ACT.Relu, bias=shift[t][:], scale=scl[t][:])
-            nc.sync.dma_start(
-                out=out[c0 // HW : (c0 + n) // HW, t * P : (t + 1) * P, :, :].rearrange("b p h w -> p b (h w)"),
-                in_=res[:].rearrange("p (b x) -> p b x", x=HW),
-            )
+                nc.sync.dma_start(
+                    out=out[c0 // HW : (c0 + n) // HW, t * P : (t + 1) * P, :, :].rearrange("b p h w -> p b (h w)"),
+                    in_=res[:].rearrange("p (b x) -> p b x", x=HW),
+                )
 
         tile_stats(0)
         quant_w(2)

@@ -12,11 +12,18 @@ ACT = mybir.ActivationFunctionType
 ALU = mybir.AluOpType
 
 P = 128
+PACK = 4
 B, C, HW, O = 5, 512, 256, 512
 NPIX = B * HW
 OT = O // P
+PASSES = 2
+BANK = 512
+L2_EPS = 1e-12
+BN_EPS = 1e-5
 FLOPS = 2 * NPIX * 2 * C * O
-CHUNKS = ((0, 512), (512, 512), (1024, 256))
+CHUNKS = ((0, BANK), (BANK, BANK), (2 * BANK, HW))
+CM_BEHIND_NORM = ((), (), (1,), (2, 3), (4,))
+VECTOR_RELU = ((2, 1), (3, 2))
 
 
 def tile_memory_sup_pb_kernel(tc, query, concat_memory, conv_w, bn_gamma, bn_beta, out):
@@ -26,36 +33,34 @@ def tile_memory_sup_pb_kernel(tc, query, concat_memory, conv_w, bn_gamma, bn_bet
         psum = ctx.enter_context(tc.psum_pool(name="psum", bufs=8))
         ctx.enter_context(tc.manual_schedule())
 
-        one1 = keep.tile([P, 1], F32, name="one1")
-        nc.vector.memset(one1[:], 1.0)
-        eps = keep.tile([P, 1], F32, name="eps")
-        nc.vector.tensor_scalar(out=eps[:], in0=one1[:], scalar1=1e-5, scalar2=None, op0=ALU.mult)
-        ones = keep.tile([P, P], F32, name="ones")
-        nc.vector.memset(ones[:], 1.0)
-        warm_ps = psum.tile([P, 512], F32, name="warm_ps", tag="bank")
-        for i in range(4):
-            nc.tensor.matmul(out=warm_ps[:, 0:P], lhsT=ones[:], rhs=ones[:], start=True, stop=True)
-        gb = keep.tile([P, P], BF16, name="gb")
-        nc.vector.memset(gb[:], 0.0)
+        one = keep.tile([P, 1], F32, name="one")
+        nc.vector.memset(one[:], 1.0)
+        bn_eps = keep.tile([P, 1], F32, name="bn_eps")
+        nc.vector.tensor_scalar(out=bn_eps[:], in0=one[:], scalar1=BN_EPS, scalar2=None, op0=ALU.mult)
+        gain_rows = keep.tile([P, P], BF16, name="gain_rows")
+        nc.vector.memset(gain_rows[:], 0.0)
         ident = keep.tile([P, P], F32, name="ident")
         make_identity(nc, ident[:])
-        nc.scalar.dma_start(out=gb[0:4, :], in_=bn_gamma.rearrange("(t p) -> t p", p=P))
-        nc.scalar.dma_start(out=gb[4:8, :], in_=bn_beta.rearrange("(t p) -> t p", p=P))
-        warm = keep.tile([P, 1], F32, name="warm")
-        nc.scalar.activation(out=warm[:], in_=one1[:], func=ACT.Abs_reciprocal_sqrt)
+        nc.scalar.dma_start(out=gain_rows[0:OT, :], in_=bn_gamma.rearrange("(t p) -> t p", p=P))
+        nc.scalar.dma_start(out=gain_rows[OT : 2 * OT, :], in_=bn_beta.rearrange("(t p) -> t p", p=P))
+        gain_rows_f32 = keep.tile([P, P], F32, name="gain_rows_f32")
+        nc.gpsimd.tensor_copy(out=gain_rows_f32[:], in_=gain_rows[:])
+        table_warm = keep.tile([P, 1], F32, name="table_warm")
+        nc.scalar.activation(out=table_warm[:], in_=one[:], func=ACT.Abs_reciprocal_sqrt)
 
-        q_view = query.rearrange("b (p j) h w -> p b j (h w)", j=4)
+        q_view = query.rearrange("b (p j) h w -> p b j (h w)", j=PACK)
         cm_view = concat_memory.rearrange("(r p) c -> p r c", p=P)
         w_view = conv_w.rearrange("(t p) k -> p t k", p=P)
-        q_raw = [keep.tile([P, 4, HW], BF16, name="q_raw%d" % b) for b in range(B)]
-        cm_raw = [keep.tile([P, 2, C], BF16, name="cm_raw%d" % g) for g in range(B)]
+        q_raw = [keep.tile([P, PACK, HW], BF16, name="q_raw%d" % b) for b in range(B)]
+        cm_raw = [keep.tile([P, HW // P, C], BF16, name="cm_raw%d" % b) for b in range(B)]
         w_raw = [keep.tile([P, 2 * C], BF16, name="w_raw%d" % t) for t in range(OT)]
 
         def load_q(b):
             nc.sync.dma_start(out=q_raw[b][:], in_=q_view[:, b, :, :])
 
-        def load_cm(g):
-            nc.sync.dma_start(out=cm_raw[g][:], in_=cm_view[:, 2 * g : 2 * g + 2, :])
+        def load_cm(b):
+            rows = HW // P
+            nc.sync.dma_start(out=cm_raw[b][:], in_=cm_view[:, rows * b : rows * (b + 1), :])
 
         def load_w(t):
             nc.sync.dma_start(out=w_raw[t][:], in_=w_view[:, t, :])
@@ -66,252 +71,235 @@ def tile_memory_sup_pb_kernel(tc, query, concat_memory, conv_w, bn_gamma, bn_bet
         load_cm(0)
         for b in range(2, B):
             load_q(b)
-        for g in range(1, B):
-            load_cm(g)
+        for b in range(1, B):
+            load_cm(b)
         for t in range(1, OT):
             load_w(t)
 
-        u_codes = keep.tile([P, 2, NPIX], U32, name="u_codes", align_bytes=64)
-        u_scales = keep.tile([P, 2, NPIX], U8, name="u_scales", align_bytes=64)
-        w_codes = keep.tile([P, OT, 2 * P], U32, name="w_codes", align_bytes=64)
-        w_scales = keep.tile([P, OT, 2 * P], U8, name="w_scales", align_bytes=64)
-        junk = keep.tile([P, 4, P], BF16, name="junk")
-        tq, ss, rn, r_t, qg = {}, {}, {}, {}, {}
-        c_t, cg, w_t, wg = {}, {}, {}, {}
+        u_codes = keep.tile([P, PASSES, NPIX], U32, name="u_codes", align_bytes=64)
+        u_scales = keep.tile([P, PASSES, NPIX], U8, name="u_scales", align_bytes=64)
+        w_codes = keep.tile([P, OT, PASSES * P], U32, name="w_codes", align_bytes=64)
+        w_scales = keep.tile([P, OT, PASSES * P], U8, name="w_scales", align_bytes=64)
+        squares = keep.tile([P, PACK, P], BF16, name="squares")
+        q_t, sum_sq, inv_norm, inv_norm_all, q_grouped = {}, {}, {}, {}, {}
+        cm_t, cm_grouped, w_t, w_grouped = {}, {}, {}, {}
 
-        def t_q(b):
-            tq[b] = psum.tile([P, 4, P], F32, name="tq%d" % b, tag="bank")
-            qw = q_raw[b][:].bitcast(F32)
-            for j in range(4):
-                nc.tensor.transpose(tq[b][:, j, :], qw[:, j, :], ident[:])
+        def transpose_q(b):
+            q_t[b] = psum.tile([P, PACK, P], F32, name="q_t%d" % b, tag="bank")
+            words = q_raw[b][:].bitcast(F32)
+            for j in range(PACK):
+                nc.tensor.transpose(q_t[b][:, j, :], words[:, j, :], ident[:])
 
-        def sq_q(b):
-            ss[b] = keep.tile([P, 2], F32, name="ss%d" % b)
-            v = tq[b][:].bitcast(BF16).rearrange("p j (c e) -> p e j c", e=2)
+        def norm_q(b):
+            sum_sq[b] = keep.tile([P, 2], F32, name="sum_sq%d" % b)
+            halves = q_t[b][:].bitcast(BF16).rearrange("m j (p e) -> m e j p", e=2)
             for e in range(2):
-                nc.scalar.activation(out=junk[:], in_=v[:, e, :, :], func=ACT.Square, accum_out=ss[b][:, e : e + 1])
-            rn[b] = keep.tile([P, 2], F32, name="rn%d" % b)
-            nc.scalar.activation(out=rn[b][:], in_=ss[b][:], func=ACT.Abs_reciprocal_sqrt)
+                nc.scalar.activation(
+                    out=squares[:], in_=halves[:, e, :, :], func=ACT.Square, accum_out=sum_sq[b][:, e : e + 1]
+                )
+            inv_norm[b] = keep.tile([P, 2], F32, name="inv_norm%d" % b)
+            nc.scalar.activation(out=inv_norm[b][:], in_=sum_sq[b][:], func=ACT.Abs_reciprocal_sqrt)
 
-        def bc_q(b):
-            r_t[b] = psum.tile([P, 512], F32, name="r_t%d" % b, tag="bank")
+        def spread_norm(b):
+            inv_norm_all[b] = psum.tile([P, BANK], F32, name="inv_norm_all%d" % b, tag="bank")
             for e in range(2):
                 nc.tensor.matmul(
-                    out=r_t[b][:, e:HW:2],
-                    lhsT=rn[b][:, e : e + 1].to_broadcast([P, P]),
+                    out=inv_norm_all[b][:, e:HW:2],
+                    lhsT=inv_norm[b][:, e : e + 1].to_broadcast([P, P]),
                     rhs=ident[:],
                     start=True,
                     stop=True,
                 )
 
-        def st_q(b):
-            qg[b] = keep.tile([P, HW, 4], BF16, name="qg%d" % b, align_bytes=64)
+        def normalise_q(b):
+            q_grouped[b] = keep.tile([P, HW, PACK], BF16, name="q_grouped%d" % b, align_bytes=64)
             nc.vector.scalar_tensor_tensor(
-                out=qg[b][:],
-                in0=r_t[b][:, 0:HW].unsqueeze(2).to_broadcast([P, HW, 4]),
-                scalar=1e12,
-                in1=q_raw[b][:].rearrange("p j w -> p w j"),
+                out=q_grouped[b][:],
+                in0=inv_norm_all[b][:, 0:HW].unsqueeze(2).to_broadcast([P, HW, PACK]),
+                scalar=1.0 / L2_EPS,
+                in1=q_raw[b][:].rearrange("p j x -> p x j"),
                 op0=ALU.min,
                 op1=ALU.mult,
             )
 
-        def qq(b):
-            cols = slice(b * HW, (b + 1) * HW)
+        def quantise_q(b):
+            pixels = slice(b * HW, (b + 1) * HW)
             nc.vector.quantize_mx(
-                out=u_codes[:, 0, cols].bitcast(FP8X4),
-                scales=u_scales[:, 0, cols],
-                in_=qg[b][:].rearrange("p w j -> p (w j)"),
+                out=u_codes[:, 0, pixels].bitcast(FP8X4),
+                scales=u_scales[:, 0, pixels],
+                in_=q_grouped[b][:].rearrange("p x j -> p (x j)"),
             )
 
-        def t_c(g):
-            c_t[g] = psum.tile([P, 2, 2, P], F32, name="c_t%d" % g, tag="bank")
-            cw = cm_raw[g][:].bitcast(F32)
-            for r in range(2):
+        def transpose_cm(b):
+            cm_t[b] = psum.tile([P, HW // P, 2, P], F32, name="cm_t%d" % b, tag="bank")
+            words = cm_raw[b][:].bitcast(F32)
+            for r in range(HW // P):
                 for u in range(2):
-                    nc.tensor.transpose(c_t[g][:, r, u, :], cw[:, r, u * P : (u + 1) * P], ident[:])
+                    nc.tensor.transpose(cm_t[b][:, r, u, :], words[:, r, u * P : (u + 1) * P], ident[:])
 
-        def cp_c(g, on_vector):
-            cg[g] = keep.tile([P, 2, P, 4], BF16, name="cg%d" % g, align_bytes=64)
-            src = c_t[g][:].rearrange("p r u x -> p r x u")
-            if on_vector:
-                nc.vector.tensor_copy(out=cg[g][:].bitcast(F32), in_=src)
-            else:
-                nc.scalar.copy(out=cg[g][:].bitcast(F32), in_=src)
+        def copy_cm(b, copy):
+            cm_grouped[b] = keep.tile([P, HW // P, P, PACK], BF16, name="cm_grouped%d" % b, align_bytes=64)
+            copy(out=cm_grouped[b][:].bitcast(F32), in_=cm_t[b][:].rearrange("p r u v -> p r v u"))
 
-        def qc(g):
-            cols = slice(g * HW, (g + 1) * HW)
+        def quantise_cm(b):
+            pixels = slice(b * HW, (b + 1) * HW)
             nc.vector.quantize_mx(
-                out=u_codes[:, 1, cols].bitcast(FP8X4),
-                scales=u_scales[:, 1, cols],
-                in_=cg[g][:].rearrange("p r x j -> p (r x j)"),
+                out=u_codes[:, 1, pixels].bitcast(FP8X4),
+                scales=u_scales[:, 1, pixels],
+                in_=cm_grouped[b][:].rearrange("p r v j -> p (r v j)"),
             )
 
-        def t_w(t):
-            w_t[t] = psum.tile([P, 2, 2, P], F32, name="w_t%d" % t, tag="bank")
-            ww = w_raw[t][:].bitcast(F32)
-            for h in range(2):
-                nc.tensor.transpose(w_t[t][:, 0, h, :], ww[:, h : 2 * P : 2], ident[:])
+        def transpose_w(t):
+            w_t[t] = psum.tile([P, PASSES, 2, P], F32, name="w_t%d" % t, tag="bank")
+            words = w_raw[t][:].bitcast(F32)
             for u in range(2):
-                nc.tensor.transpose(w_t[t][:, 1, u, :], ww[:, (2 + u) * P : (3 + u) * P], ident[:])
+                nc.tensor.transpose(w_t[t][:, 0, u, :], words[:, u : 2 * P : 2], ident[:])
+            for u in range(2):
+                nc.tensor.transpose(w_t[t][:, 1, u, :], words[:, (2 + u) * P : (3 + u) * P], ident[:])
 
-        def cp_w(t, on_vector):
-            wg[t] = keep.tile([P, 2, P, 4], BF16, name="wg%d" % t, align_bytes=64)
-            src = w_t[t][:].rearrange("p c u o -> p c o u")
-            if on_vector:
-                nc.vector.tensor_copy(out=wg[t][:].bitcast(F32), in_=src)
-            else:
-                nc.scalar.copy(out=wg[t][:].bitcast(F32), in_=src)
+        def copy_w(t, copy):
+            w_grouped[t] = keep.tile([P, PASSES, P, PACK], BF16, name="w_grouped%d" % t, align_bytes=64)
+            copy(out=w_grouped[t][:].bitcast(F32), in_=w_t[t][:].rearrange("p a u o -> p a o u"))
 
-        def quant_w(t):
+        def quantise_w(t):
             nc.vector.quantize_mx(
                 out=w_codes[:, t, :].bitcast(FP8X4),
                 scales=w_scales[:, t, :],
-                in_=wg[t][:].rearrange("p c o j -> p (c o j)"),
+                in_=w_grouped[t][:].rearrange("p a o j -> p (a o j)"),
             )
 
-        t_q(0)
-        t_w(0)
-        t_q(1)
-        t_c(0)
-        sq_q(0)
-        cp_w(0, True)
-        cp_c(0, True)
-        quant_w(0)
-        qc(0)
-        bc_q(0)
-        t_q(2)
-        sq_q(1)
-        st_q(0)
-        bc_q(1)
-        t_q(3)
-        sq_q(2)
-        st_q(1)
-        qq(0)
-        gbf = keep.tile([P, P], F32, name="gbf")
-        nc.vector.tensor_copy(out=gbf[:], in_=gb[:])
-        bc_q(2)
-        t_q(4)
-        t_c(1)
-        sq_q(3)
-        st_q(2)
-        qq(1)
-        bc_q(3)
-        t_c(2)
-        t_c(3)
-        sq_q(4)
-        st_q(3)
-        qq(2)
-        bc_q(4)
-        t_c(4)
+        transpose_q(0)
+        transpose_w(0)
+        transpose_q(1)
+        transpose_cm(0)
+        norm_q(0)
+        copy_w(0, nc.vector.tensor_copy)
+        copy_cm(0, nc.vector.tensor_copy)
+        quantise_w(0)
+        quantise_cm(0)
+        for b in range(B):
+            spread_norm(b)
+            if b + 2 < B:
+                transpose_q(b + 2)
+            for later in CM_BEHIND_NORM[b]:
+                transpose_cm(later)
+            if b + 1 < B:
+                norm_q(b + 1)
+            normalise_q(b)
+            if b >= 1:
+                quantise_q(b - 1)
         for t in range(1, OT):
-            t_w(t)
-        g_t = psum.tile([P, 512], F32, name="g_t", tag="bank")
-        nc.tensor.transpose(g_t[:, 0:P], gbf[:], ident[:])
-        for g in range(1, B):
-            cp_c(g, False)
+            transpose_w(t)
+        gain_t = psum.tile([P, BANK], F32, name="gain_t", tag="bank")
+        nc.tensor.transpose(gain_t[:, 0:P], gain_rows_f32[:], ident[:])
+        for b in range(1, B):
+            copy_cm(b, nc.scalar.copy)
         for t in range(1, OT):
-            cp_w(t, False)
-        gbt = keep.tile([P, 8], F32, name="gbt")
-        nc.scalar.copy(out=gbt[:], in_=g_t[:, 0:8])
-        ngam = keep.tile([P, 4], F32, name="ngam")
-        nc.scalar.activation(out=ngam[:], in_=g_t[:, 0:4], func=ACT.Copy, scale=-1.0)
-        st_q(4)
-        qq(3)
-        qc(1)
-        qq(4)
-        qc(2)
-        qc(3)
-        qc(4)
-        quant_w(1)
+            copy_w(t, nc.scalar.copy)
+        gain = keep.tile([P, 2 * OT], F32, name="gain")
+        nc.scalar.copy(out=gain[:], in_=gain_t[:, 0 : 2 * OT])
+        neg_gamma = keep.tile([P, OT], F32, name="neg_gamma")
+        nc.scalar.activation(out=neg_gamma[:], in_=gain_t[:, 0:OT], func=ACT.Copy, scale=-1.0)
+        quantise_cm(1)
+        quantise_q(B - 1)
+        for b in range(2, B):
+            quantise_cm(b)
+        quantise_w(1)
 
-        ys, stats, mv, rstd, nmg, scl, shift = {}, {}, {}, {}, {}, {}, {}
+        y, stats, mean_var, rstd, neg_mean_gamma, bn_scale, bn_shift = {}, {}, {}, {}, {}, {}, {}
 
-        def mx(t, i):
-            c0, n = CHUNKS[i]
-            ys[(t, i)] = psum.tile([P, 512], F32, name="y%d_%d" % (t, i), tag="bank")
-            for c in range(2):
-                nc.tensor.matmul_mx(
-                    out=ys[(t, i)][:, 0:n],
-                    lhsT=w_codes[:, t, c * P : (c + 1) * P].bitcast(FP8X4),
-                    lhsT_scale=w_scales[:, t, c * P : (c + 1) * P],
-                    rhs=u_codes[:, c, c0 : c0 + n].bitcast(FP8X4),
-                    rhs_scale=u_scales[:, c, c0 : c0 + n],
-                    start=(c == 0),
-                    stop=(c == 1),
-                )
+        def statistics(t):
+            stats[t] = keep.tile([P, len(CHUNKS), 6], F32, name="stats%d" % t)
+            for i, (first, n) in enumerate(CHUNKS):
+                y[(t, i)] = psum.tile([P, BANK], F32, name="y%d_%d" % (t, i), tag="bank")
+                for a in range(PASSES):
+                    nc.tensor.matmul_mx(
+                        out=y[(t, i)][:, 0:n],
+                        lhsT=w_codes[:, t, a * P : (a + 1) * P].bitcast(FP8X4),
+                        lhsT_scale=w_scales[:, t, a * P : (a + 1) * P],
+                        rhs=u_codes[:, a, first : first + n].bitcast(FP8X4),
+                        rhs_scale=u_scales[:, a, first : first + n],
+                        start=(a == 0),
+                        stop=(a == PASSES - 1),
+                    )
+                nc.vector.bn_stats(out=stats[t][:, i, :], in_=y[(t, i)][:, 0:n])
 
-        def tile_stats(t):
-            stats[t] = keep.tile([P, 3, 6], F32, name="stats%d" % t)
-            for i in range(3):
-                mx(t, i)
-                nc.vector.bn_stats(out=stats[t][:, i, :], in_=ys[(t, i)][:, 0 : CHUNKS[i][1]])
+        def aggregate(t):
+            mean_var[t] = keep.tile([P, 2], F32, name="mean_var%d" % t)
+            nc.vector.bn_aggr(out=mean_var[t][:], in_=stats[t][:].rearrange("p i s -> p (i s)"))
 
-        def aggr(t):
-            mv[t] = keep.tile([P, 2], F32, name="mv%d" % t)
-            nc.vector.bn_aggr(out=mv[t][:], in_=stats[t][:].rearrange("p a s -> p (a s)"))
-
-        def chain_a(t):
+        def chain_first(t):
             rstd[t] = keep.tile([P, 1], F32, name="rstd%d" % t)
-            nc.scalar.activation(out=rstd[t][:], in_=mv[t][:, 1:2], func=ACT.Abs_reciprocal_sqrt, bias=eps[:])
-            nmg[t] = keep.tile([P, 1], F32, name="nmg%d" % t)
-            nc.scalar.activation(out=nmg[t][:], in_=mv[t][:, 0:1], func=ACT.Copy, scale=ngam[:, t : t + 1])
-
-        def chain_b(t):
-            scl[t] = keep.tile([P, 1], F32, name="scl%d" % t)
-            nc.scalar.activation(out=scl[t][:], in_=rstd[t][:], func=ACT.Copy, scale=gbt[:, t : t + 1])
-            shift[t] = keep.tile([P, 1], F32, name="shift%d" % t)
             nc.scalar.activation(
-                out=shift[t][:], in_=rstd[t][:], func=ACT.Identity, scale=nmg[t][:], bias=gbt[:, 4 + t : 5 + t]
+                out=rstd[t][:], in_=mean_var[t][:, 1:2], func=ACT.Abs_reciprocal_sqrt, bias=bn_eps[:]
+            )
+            neg_mean_gamma[t] = keep.tile([P, 1], F32, name="neg_mean_gamma%d" % t)
+            nc.scalar.activation(
+                out=neg_mean_gamma[t][:], in_=mean_var[t][:, 0:1], func=ACT.Copy, scale=neg_gamma[:, t : t + 1]
             )
 
-        def relu(t, i, on_vector):
-            c0, n = CHUNKS[i]
-            res = keep.tile([P, n], F32, name="res%d_%d" % (t, i))
-            if on_vector:
-                for h in range(0, n, HW):
-                    nc.vector.tensor_scalar(
-                        out=res[:, h : h + HW],
-                        in0=ys[(t, i)][:, h : h + HW],
-                        scalar1=scl[t][:],
-                        scalar2=shift[t][:],
-                        op0=ALU.mult,
-                        op1=ALU.add,
-                    )
-                for h in range(0, n, HW):
-                    nc.vector.tensor_scalar(
-                        out=res[:, h : h + HW], in0=res[:, h : h + HW], scalar1=0.0, scalar2=None, op0=ALU.max
-                    )
-                    nc.sync.dma_start(
-                        out=out[(c0 + h) // HW, t * P : (t + 1) * P, :, :].rearrange("p h w -> p (h w)"),
-                        in_=res[:, h : h + HW],
-                    )
-            else:
-                nc.scalar.activation(out=res[:], in_=ys[(t, i)][:, 0:n], func=ACT.Relu, bias=shift[t][:], scale=scl[t][:])
-                nc.sync.dma_start(
-                    out=out[c0 // HW : (c0 + n) // HW, t * P : (t + 1) * P, :, :].rearrange("b p h w -> p b (h w)"),
-                    in_=res[:].rearrange("p (b x) -> p b x", x=HW),
-                )
+        def chain_second(t):
+            bn_scale[t] = keep.tile([P, 1], F32, name="bn_scale%d" % t)
+            nc.scalar.activation(out=bn_scale[t][:], in_=rstd[t][:], func=ACT.Copy, scale=gain[:, t : t + 1])
+            bn_shift[t] = keep.tile([P, 1], F32, name="bn_shift%d" % t)
+            nc.scalar.activation(
+                out=bn_shift[t][:],
+                in_=rstd[t][:],
+                func=ACT.Identity,
+                scale=neg_mean_gamma[t][:],
+                bias=gain[:, OT + t : OT + t + 1],
+            )
 
-        tile_stats(0)
-        quant_w(2)
-        aggr(0)
-        chain_a(0)
-        chain_b(0)
-        tile_stats(1)
-        quant_w(3)
-        aggr(1)
-        for t in range(OT - 1):
-            relu(t, 0, False)
-            relu(t, 1, False)
-            chain_a(t + 1)
+        def store(t, first, n, result):
+            nc.sync.dma_start(
+                out=out[first // HW : (first + n) // HW, t * P : (t + 1) * P, :, :].rearrange("b p h w -> p b (h w)"),
+                in_=result.rearrange("p (b x) -> p b x", x=HW),
+            )
+
+        def relu_scalar(t, i):
+            first, n = CHUNKS[i]
+            result = keep.tile([P, n], F32, name="result%d_%d" % (t, i))
+            nc.scalar.activation(
+                out=result[:], in_=y[(t, i)][:, 0:n], func=ACT.Relu, bias=bn_shift[t][:], scale=bn_scale[t][:]
+            )
+            store(t, first, n, result[:])
+
+        def relu_vector(t, i):
+            first, n = CHUNKS[i]
+            result = keep.tile([P, n], F32, name="result%d_%d" % (t, i))
+            for x0 in range(0, n, HW):
+                nc.vector.tensor_scalar(
+                    out=result[:, x0 : x0 + HW],
+                    in0=y[(t, i)][:, x0 : x0 + HW],
+                    scalar1=bn_scale[t][:],
+                    scalar2=bn_shift[t][:],
+                    op0=ALU.mult,
+                    op1=ALU.add,
+                )
+            for x0 in range(0, n, HW):
+                nc.vector.tensor_scalar(
+                    out=result[:, x0 : x0 + HW], in0=result[:, x0 : x0 + HW], scalar1=0.0, scalar2=None, op0=ALU.max
+                )
+                store(t, first + x0, HW, result[:, x0 : x0 + HW])
+
+        statistics(0)
+        quantise_w(2)
+        aggregate(0)
+        chain_first(0)
+        chain_second(0)
+        statistics(1)
+        quantise_w(3)
+        aggregate(1)
+        for t in range(OT):
+            for i in range(len(CHUNKS)):
+                if i == len(CHUNKS) - 1 and t + 1 < OT:
+                    chain_first(t + 1)
+                if (t, i) in VECTOR_RELU:
+                    relu_vector(t, i)
+                else:
+                    relu_scalar(t, i)
+            if t + 1 < OT:
+                chain_second(t + 1)
             if t + 2 < OT:
-                relu(t, 2, False)
-                chain_b(t + 1)
-                tile_stats(t + 2)
-                aggr(t + 2)
-            else:
-                relu(t, 2, True)
-                chain_b(t + 1)
-        relu(OT - 1, 0, False)
-        relu(OT - 1, 2, False)
-        relu(OT - 1, 1, True)
+                statistics(t + 2)
+                aggregate(t + 2)

@@ -13,11 +13,16 @@ ALU = mybir.AluOpType
 
 P = 128
 PACK = 4
+PAIR = 2
+PLANES = PACK // PAIR
 B, C, HW, O = 5, 512, 256, 512
 NPIX = B * HW
+ROW_TILES = HW // P
 OT = O // P
 PASSES = 2
 BANK = 512
+WORDS = C // 2
+BN_STATS = 6
 L2_EPS = 1e-12
 BN_EPS = 1e-5
 FLOPS = 2 * NPIX * 2 * C * O
@@ -52,15 +57,14 @@ def tile_memory_sup_pb_kernel(tc, query, concat_memory, conv_w, bn_gamma, bn_bet
         cm_view = concat_memory.rearrange("(r p) c -> p r c", p=P)
         w_view = conv_w.rearrange("(t p) k -> p t k", p=P)
         q_raw = [keep.tile([P, PACK, HW], BF16, name="q_raw%d" % b) for b in range(B)]
-        cm_raw = [keep.tile([P, HW // P, C], BF16, name="cm_raw%d" % b) for b in range(B)]
-        w_raw = [keep.tile([P, 2 * C], BF16, name="w_raw%d" % t) for t in range(OT)]
+        cm_raw = [keep.tile([P, ROW_TILES, C], BF16, name="cm_raw%d" % b) for b in range(B)]
+        w_raw = [keep.tile([P, PASSES * C], BF16, name="w_raw%d" % t) for t in range(OT)]
 
         def load_q(b):
             nc.sync.dma_start(out=q_raw[b][:], in_=q_view[:, b, :, :])
 
         def load_cm(b):
-            rows = HW // P
-            nc.sync.dma_start(out=cm_raw[b][:], in_=cm_view[:, rows * b : rows * (b + 1), :])
+            nc.sync.dma_start(out=cm_raw[b][:], in_=cm_view[:, ROW_TILES * b : ROW_TILES * (b + 1), :])
 
         def load_w(t):
             nc.sync.dma_start(out=w_raw[t][:], in_=w_view[:, t, :])
@@ -91,20 +95,20 @@ def tile_memory_sup_pb_kernel(tc, query, concat_memory, conv_w, bn_gamma, bn_bet
                 nc.tensor.transpose(q_t[b][:, j, :], words[:, j, :], ident[:])
 
         def norm_q(b):
-            sum_sq[b] = keep.tile([P, 2], F32, name="sum_sq%d" % b)
-            halves = q_t[b][:].bitcast(BF16).rearrange("m j (p e) -> m e j p", e=2)
-            for e in range(2):
+            sum_sq[b] = keep.tile([P, PAIR], F32, name="sum_sq%d" % b)
+            halves = q_t[b][:].bitcast(BF16).rearrange("m j (p e) -> m e j p", e=PAIR)
+            for e in range(PAIR):
                 nc.scalar.activation(
                     out=squares[:], in_=halves[:, e, :, :], func=ACT.Square, accum_out=sum_sq[b][:, e : e + 1]
                 )
-            inv_norm[b] = keep.tile([P, 2], F32, name="inv_norm%d" % b)
+            inv_norm[b] = keep.tile([P, PAIR], F32, name="inv_norm%d" % b)
             nc.scalar.activation(out=inv_norm[b][:], in_=sum_sq[b][:], func=ACT.Abs_reciprocal_sqrt)
 
         def spread_norm(b):
             inv_norm_all[b] = psum.tile([P, BANK], F32, name="inv_norm_all%d" % b, tag="bank")
-            for e in range(2):
+            for e in range(PAIR):
                 nc.tensor.matmul(
-                    out=inv_norm_all[b][:, e:HW:2],
+                    out=inv_norm_all[b][:, e:HW:PAIR],
                     lhsT=inv_norm[b][:, e : e + 1].to_broadcast([P, P]),
                     rhs=ident[:],
                     start=True,
@@ -131,14 +135,14 @@ def tile_memory_sup_pb_kernel(tc, query, concat_memory, conv_w, bn_gamma, bn_bet
             )
 
         def transpose_cm(b):
-            cm_t[b] = psum.tile([P, HW // P, 2, P], F32, name="cm_t%d" % b, tag="bank")
+            cm_t[b] = psum.tile([P, ROW_TILES, PLANES, P], F32, name="cm_t%d" % b, tag="bank")
             words = cm_raw[b][:].bitcast(F32)
-            for r in range(HW // P):
-                for u in range(2):
+            for r in range(ROW_TILES):
+                for u in range(PLANES):
                     nc.tensor.transpose(cm_t[b][:, r, u, :], words[:, r, u * P : (u + 1) * P], ident[:])
 
         def copy_cm(b, copy):
-            cm_grouped[b] = keep.tile([P, HW // P, P, PACK], BF16, name="cm_grouped%d" % b, align_bytes=64)
+            cm_grouped[b] = keep.tile([P, ROW_TILES, P, PACK], BF16, name="cm_grouped%d" % b, align_bytes=64)
             copy(out=cm_grouped[b][:].bitcast(F32), in_=cm_t[b][:].rearrange("p r u v -> p r v u"))
 
         def quantise_cm(b):
@@ -150,12 +154,12 @@ def tile_memory_sup_pb_kernel(tc, query, concat_memory, conv_w, bn_gamma, bn_bet
             )
 
         def transpose_w(t):
-            w_t[t] = psum.tile([P, PASSES, 2, P], F32, name="w_t%d" % t, tag="bank")
+            w_t[t] = psum.tile([P, PASSES, PLANES, P], F32, name="w_t%d" % t, tag="bank")
             words = w_raw[t][:].bitcast(F32)
-            for u in range(2):
-                nc.tensor.transpose(w_t[t][:, 0, u, :], words[:, u : 2 * P : 2], ident[:])
-            for u in range(2):
-                nc.tensor.transpose(w_t[t][:, 1, u, :], words[:, (2 + u) * P : (3 + u) * P], ident[:])
+            for u in range(PLANES):
+                nc.tensor.transpose(w_t[t][:, 0, u, :], words[:, u:WORDS:PLANES], ident[:])
+            for u in range(PLANES):
+                nc.tensor.transpose(w_t[t][:, 1, u, :], words[:, WORDS + u * P : WORDS + (u + 1) * P], ident[:])
 
         def copy_w(t, copy):
             w_grouped[t] = keep.tile([P, PASSES, P, PACK], BF16, name="w_grouped%d" % t, align_bytes=64)
@@ -185,9 +189,9 @@ def tile_memory_sup_pb_kernel(tc, query, concat_memory, conv_w, bn_gamma, bn_bet
                 transpose_cm(later)
             if b + 1 < B:
                 norm_q(b + 1)
-            normalise_q(b)
-            if b >= 1:
-                quantise_q(b - 1)
+                normalise_q(b)
+                if b >= 1:
+                    quantise_q(b - 1)
         for t in range(1, OT):
             transpose_w(t)
         gain_t = psum.tile([P, BANK], F32, name="gain_t", tag="bank")
@@ -201,15 +205,18 @@ def tile_memory_sup_pb_kernel(tc, query, concat_memory, conv_w, bn_gamma, bn_bet
         neg_gamma = keep.tile([P, OT], F32, name="neg_gamma")
         nc.scalar.activation(out=neg_gamma[:], in_=gain_t[:, 0:OT], func=ACT.Copy, scale=-1.0)
         quantise_cm(1)
+        normalise_q(B - 1)
+        quantise_q(B - 2)
+        quantise_cm(2)
+        quantise_cm(3)
         quantise_q(B - 1)
-        for b in range(2, B):
-            quantise_cm(b)
+        quantise_cm(4)
         quantise_w(1)
 
         y, stats, mean_var, rstd, neg_mean_gamma, bn_scale, bn_shift = {}, {}, {}, {}, {}, {}, {}
 
         def statistics(t):
-            stats[t] = keep.tile([P, len(CHUNKS), 6], F32, name="stats%d" % t)
+            stats[t] = keep.tile([P, len(CHUNKS), BN_STATS], F32, name="stats%d" % t)
             for i, (first, n) in enumerate(CHUNKS):
                 y[(t, i)] = psum.tile([P, BANK], F32, name="y%d_%d" % (t, i), tag="bank")
                 for a in range(PASSES):

from contextlib import ExitStack

import concourse.mybir as mybir
from concourse.masks import make_identity

F32 = mybir.dt.float32
BF16 = mybir.dt.bfloat16
U32 = mybir.dt.uint32
U8 = mybir.dt.uint8
FP8X4 = mybir.dt.float8_e4m3fn_x4
ACT = mybir.ActivationFunctionType
ALU = mybir.AluOpType

P = 128
PACK = 4
PAIR = 2
PLANES = PACK // PAIR
B, C, HW, O = 5, 512, 256, 512
NPIX = B * HW
ROW_TILES = HW // P
OT = O // P
PASSES = 2
BANK = 512
WORDS = C // 2
BN_STATS = 6
L2_EPS = 1e-12
BN_EPS = 1e-5
FLOPS = 2 * NPIX * 2 * C * O
CHUNKS = ((0, BANK), (BANK, BANK), (2 * BANK, HW))
CM_BEHIND_NORM = ((), (), (1,), (2, 3), (4,))
VECTOR_RELU = ((2, 1), (3, 2))


def tile_memory_sup_pb_kernel(tc, query, concat_memory, conv_w, bn_gamma, bn_beta, out):
    nc = tc.nc
    with ExitStack() as ctx:
        keep = ctx.enter_context(tc.tile_pool(name="keep", bufs=1))
        psum = ctx.enter_context(tc.psum_pool(name="psum", bufs=8))
        ctx.enter_context(tc.manual_schedule())

        one = keep.tile([P, 1], F32, name="one")
        nc.vector.memset(one[:], 1.0)
        bn_eps = keep.tile([P, 1], F32, name="bn_eps")
        nc.vector.tensor_scalar(out=bn_eps[:], in0=one[:], scalar1=BN_EPS, scalar2=None, op0=ALU.mult)
        gain_rows = keep.tile([P, P], BF16, name="gain_rows")
        nc.vector.memset(gain_rows[:], 0.0)
        ident = keep.tile([P, P], F32, name="ident")
        make_identity(nc, ident[:])
        nc.scalar.dma_start(out=gain_rows[0:OT, :], in_=bn_gamma.rearrange("(t p) -> t p", p=P))
        nc.scalar.dma_start(out=gain_rows[OT : 2 * OT, :], in_=bn_beta.rearrange("(t p) -> t p", p=P))
        gain_rows_f32 = keep.tile([P, P], F32, name="gain_rows_f32")
        nc.gpsimd.tensor_copy(out=gain_rows_f32[:], in_=gain_rows[:])
        table_warm = keep.tile([P, 1], F32, name="table_warm")
        nc.scalar.activation(out=table_warm[:], in_=one[:], func=ACT.Abs_reciprocal_sqrt)

        q_view = query.rearrange("b (p j) h w -> p b j (h w)", j=PACK)
        cm_view = concat_memory.rearrange("(r p) c -> p r c", p=P)
        w_view = conv_w.rearrange("(t p) k -> p t k", p=P)
        q_raw = [keep.tile([P, PACK, HW], BF16, name="q_raw%d" % b) for b in range(B)]
        cm_raw = [keep.tile([P, ROW_TILES, C], BF16, name="cm_raw%d" % b) for b in range(B)]
        w_raw = [keep.tile([P, PASSES * C], BF16, name="w_raw%d" % t) for t in range(OT)]

        def load_q(b):
            nc.sync.dma_start(out=q_raw[b][:], in_=q_view[:, b, :, :])

        def load_cm(b):
            nc.sync.dma_start(out=cm_raw[b][:], in_=cm_view[:, ROW_TILES * b : ROW_TILES * (b + 1), :])

        def load_w(t):
            nc.sync.dma_start(out=w_raw[t][:], in_=w_view[:, t, :])

        load_q(0)
        load_w(0)
        load_q(1)
        load_cm(0)
        for b in range(2, B):
            load_q(b)
        for b in range(1, B):
            load_cm(b)
        for t in range(1, OT):
            load_w(t)

        u_codes = keep.tile([P, PASSES, NPIX], U32, name="u_codes", align_bytes=64)
        u_scales = keep.tile([P, PASSES, NPIX], U8, name="u_scales", align_bytes=64)
        w_codes = keep.tile([P, OT, PASSES * P], U32, name="w_codes", align_bytes=64)
        w_scales = keep.tile([P, OT, PASSES * P], U8, name="w_scales", align_bytes=64)
        squares = keep.tile([P, PACK, P], BF16, name="squares")
        q_t, sum_sq, inv_norm, inv_norm_all, q_grouped = {}, {}, {}, {}, {}
        cm_t, cm_grouped, w_t, w_grouped = {}, {}, {}, {}

        def transpose_q(b):
            q_t[b] = psum.tile([P, PACK, P], F32, name="q_t%d" % b, tag="bank")
            words = q_raw[b][:].bitcast(F32)
            for j in range(PACK):
                nc.tensor.transpose(q_t[b][:, j, :], words[:, j, :], ident[:])

        def norm_q(b):
            sum_sq[b] = keep.tile([P, PAIR], F32, name="sum_sq%d" % b)
            halves = q_t[b][:].bitcast(BF16).rearrange("m j (p e) -> m e j p", e=PAIR)
            for e in range(PAIR):
                nc.scalar.activation(
                    out=squares[:], in_=halves[:, e, :, :], func=ACT.Square, accum_out=sum_sq[b][:, e : e + 1]
                )
            inv_norm[b] = keep.tile([P, PAIR], F32, name="inv_norm%d" % b)
            nc.scalar.activation(out=inv_norm[b][:], in_=sum_sq[b][:], func=ACT.Abs_reciprocal_sqrt)

        def spread_norm(b):
            inv_norm_all[b] = psum.tile([P, BANK], F32, name="inv_norm_all%d" % b, tag="bank")
            for e in range(PAIR):
                nc.tensor.matmul(
                    out=inv_norm_all[b][:, e:HW:PAIR],
                    lhsT=inv_norm[b][:, e : e + 1].to_broadcast([P, P]),
                    rhs=ident[:],
                    start=True,
                    stop=True,
                )

        def normalise_q(b):
            q_grouped[b] = keep.tile([P, HW, PACK], BF16, name="q_grouped%d" % b, align_bytes=64)
            nc.vector.scalar_tensor_tensor(
                out=q_grouped[b][:],
                in0=inv_norm_all[b][:, 0:HW].unsqueeze(2).to_broadcast([P, HW, PACK]),
                scalar=1.0 / L2_EPS,
                in1=q_raw[b][:].rearrange("p j x -> p x j"),
                op0=ALU.min,
                op1=ALU.mult,
            )

        def quantise_q(b):
            pixels = slice(b * HW, (b + 1) * HW)
            nc.vector.quantize_mx(
                out=u_codes[:, 0, pixels].bitcast(FP8X4),
                scales=u_scales[:, 0, pixels],
                in_=q_grouped[b][:].rearrange("p x j -> p (x j)"),
            )

        def transpose_cm(b):
            cm_t[b] = psum.tile([P, ROW_TILES, PLANES, P], F32, name="cm_t%d" % b, tag="bank")
            words = cm_raw[b][:].bitcast(F32)
            for r in range(ROW_TILES):
                for u in range(PLANES):
                    nc.tensor.transpose(cm_t[b][:, r, u, :], words[:, r, u * P : (u + 1) * P], ident[:])

        def copy_cm(b, copy):
            cm_grouped[b] = keep.tile([P, ROW_TILES, P, PACK], BF16, name="cm_grouped%d" % b, align_bytes=64)
            copy(out=cm_grouped[b][:].bitcast(F32), in_=cm_t[b][:].rearrange("p r u v -> p r v u"))

        def quantise_cm(b):
            pixels = slice(b * HW, (b + 1) * HW)
            nc.vector.quantize_mx(
                out=u_codes[:, 1, pixels].bitcast(FP8X4),
                scales=u_scales[:, 1, pixels],
                in_=cm_grouped[b][:].rearrange("p r v j -> p (r v j)"),
            )

        def transpose_w(t):
            w_t[t] = psum.tile([P, PASSES, PLANES, P], F32, name="w_t%d" % t, tag="bank")
            words = w_raw[t][:].bitcast(F32)
            for u in range(PLANES):
                nc.tensor.transpose(w_t[t][:, 0, u, :], words[:, u:WORDS:PLANES], ident[:])
            for u in range(PLANES):
                nc.tensor.transpose(w_t[t][:, 1, u, :], words[:, WORDS + u * P : WORDS + (u + 1) * P], ident[:])

        def copy_w(t, copy):
            w_grouped[t] = keep.tile([P, PASSES, P, PACK], BF16, name="w_grouped%d" % t, align_bytes=64)
            copy(out=w_grouped[t][:].bitcast(F32), in_=w_t[t][:].rearrange("p a u o -> p a o u"))

        def quantise_w(t):
            nc.vector.quantize_mx(
                out=w_codes[:, t, :].bitcast(FP8X4),
                scales=w_scales[:, t, :],
                in_=w_grouped[t][:].rearrange("p a o j -> p (a o j)"),
            )

        transpose_q(0)
        transpose_w(0)
        transpose_q(1)
        transpose_cm(0)
        norm_q(0)
        copy_w(0, nc.vector.tensor_copy)
        copy_cm(0, nc.vector.tensor_copy)
        quantise_w(0)
        quantise_cm(0)
        for b in range(B):
            spread_norm(b)
            if b + 2 < B:
                transpose_q(b + 2)
            for later in CM_BEHIND_NORM[b]:
                transpose_cm(later)
            if b + 1 < B:
                norm_q(b + 1)
                normalise_q(b)
                if b >= 1:
                    quantise_q(b - 1)
        for t in range(1, OT):
            transpose_w(t)
        gain_t = psum.tile([P, BANK], F32, name="gain_t", tag="bank")
        nc.tensor.transpose(gain_t[:, 0:P], gain_rows_f32[:], ident[:])
        for b in range(1, B):
            copy_cm(b, nc.scalar.copy)
        for t in range(1, OT):
            copy_w(t, nc.scalar.copy)
        gain = keep.tile([P, 2 * OT], F32, name="gain")
        nc.scalar.copy(out=gain[:], in_=gain_t[:, 0 : 2 * OT])
        neg_gamma = keep.tile([P, OT], F32, name="neg_gamma")
        nc.scalar.activation(out=neg_gamma[:], in_=gain_t[:, 0:OT], func=ACT.Copy, scale=-1.0)
        quantise_cm(1)
        normalise_q(B - 1)
        quantise_q(B - 2)
        quantise_cm(2)
        quantise_cm(3)
        quantise_q(B - 1)
        quantise_cm(4)
        quantise_w(1)

        y, stats, mean_var, rstd, neg_mean_gamma, bn_scale, bn_shift = {}, {}, {}, {}, {}, {}, {}

        def statistics(t):
            stats[t] = keep.tile([P, len(CHUNKS), BN_STATS], F32, name="stats%d" % t)
            for i, (first, n) in enumerate(CHUNKS):
                y[(t, i)] = psum.tile([P, BANK], F32, name="y%d_%d" % (t, i), tag="bank")
                for a in range(PASSES):
                    nc.tensor.matmul_mx(
                        out=y[(t, i)][:, 0:n],
                        lhsT=w_codes[:, t, a * P : (a + 1) * P].bitcast(FP8X4),
                        lhsT_scale=w_scales[:, t, a * P : (a + 1) * P],
                        rhs=u_codes[:, a, first : first + n].bitcast(FP8X4),
                        rhs_scale=u_scales[:, a, first : first + n],
                        start=(a == 0),
                        stop=(a == PASSES - 1),
                    )
                nc.vector.bn_stats(out=stats[t][:, i, :], in_=y[(t, i)][:, 0:n])

        def aggregate(t):
            mean_var[t] = keep.tile([P, 2], F32, name="mean_var%d" % t)
            nc.vector.bn_aggr(out=mean_var[t][:], in_=stats[t][:].rearrange("p i s -> p (i s)"))

        def chain_first(t):
            rstd[t] = keep.tile([P, 1], F32, name="rstd%d" % t)
            nc.scalar.activation(
                out=rstd[t][:], in_=mean_var[t][:, 1:2], func=ACT.Abs_reciprocal_sqrt, bias=bn_eps[:]
            )
            neg_mean_gamma[t] = keep.tile([P, 1], F32, name="neg_mean_gamma%d" % t)
            nc.scalar.activation(
                out=neg_mean_gamma[t][:], in_=mean_var[t][:, 0:1], func=ACT.Copy, scale=neg_gamma[:, t : t + 1]
            )

        def chain_second(t):
            bn_scale[t] = keep.tile([P, 1], F32, name="bn_scale%d" % t)
            nc.scalar.activation(out=bn_scale[t][:], in_=rstd[t][:], func=ACT.Copy, scale=gain[:, t : t + 1])
            bn_shift[t] = keep.tile([P, 1], F32, name="bn_shift%d" % t)
            nc.scalar.activation(
                out=bn_shift[t][:],
                in_=rstd[t][:],
                func=ACT.Identity,
                scale=neg_mean_gamma[t][:],
                bias=gain[:, OT + t : OT + t + 1],
            )

        def store(t, first, n, result):
            nc.sync.dma_start(
                out=out[first // HW : (first + n) // HW, t * P : (t + 1) * P, :, :].rearrange("b p h w -> p b (h w)"),
                in_=result.rearrange("p (b x) -> p b x", x=HW),
            )

        def relu_scalar(t, i):
            first, n = CHUNKS[i]
            result = keep.tile([P, n], F32, name="result%d_%d" % (t, i))
            nc.scalar.activation(
                out=result[:], in_=y[(t, i)][:, 0:n], func=ACT.Relu, bias=bn_shift[t][:], scale=bn_scale[t][:]
            )
            store(t, first, n, result[:])

        def relu_vector(t, i):
            first, n = CHUNKS[i]
            result = keep.tile([P, n], F32, name="result%d_%d" % (t, i))
            for x0 in range(0, n, HW):
                nc.vector.tensor_scalar(
                    out=result[:, x0 : x0 + HW],
                    in0=y[(t, i)][:, x0 : x0 + HW],
                    scalar1=bn_scale[t][:],
                    scalar2=bn_shift[t][:],
                    op0=ALU.mult,
                    op1=ALU.add,
                )
            for x0 in range(0, n, HW):
                nc.vector.tensor_scalar(
                    out=result[:, x0 : x0 + HW], in0=result[:, x0 : x0 + HW], scalar1=0.0, scalar2=None, op0=ALU.max
                )
                store(t, first + x0, HW, result[:, x0 : x0 + HW])

        statistics(0)
        quantise_w(2)
        aggregate(0)
        chain_first(0)
        chain_second(0)
        statistics(1)
        quantise_w(3)
        aggregate(1)
        for t in range(OT):
            for i in range(len(CHUNKS)):
                if i == len(CHUNKS) - 1 and t + 1 < OT:
                    chain_first(t + 1)
                if (t, i) in VECTOR_RELU:
                    relu_vector(t, i)
                else:
                    relu_scalar(t, i)
            if t + 1 < OT:
                chain_second(t + 1)
            if t + 2 < OT:
                statistics(t + 2)
                aggregate(t + 2)
